import numpy as np
import ml_dtypes

BF16 = ml_dtypes.bfloat16


def bf(x):
    return np.asarray(x, np.float32).astype(BF16)


def f32(x):
    return np.asarray(x, np.float32)


def f64(x):
    return np.asarray(x).astype(np.float64)


def striped(idx):
    return np.tile(idx.reshape(-1, 16).T, (8, 1))


D, V, N = 512, 1024, 128
EPS = 1.1920928955078125e-07


def silu(v):
    return v / (1.0 + np.exp(-v))


def setup_inputs():
    return {
        "emb": f32(np.random.standard_normal((D, V))),
        "pos_emb": f32(np.random.standard_normal((D, N))),
        "norm_w": f32(1.0 + 0.1 * np.random.standard_normal((D, 1))),
        "w_gate": bf(np.random.standard_normal((D, D)) / np.sqrt(D)),
        "b_gate": f32(0.1 * np.random.standard_normal((D, 1))),
        "w_up": bf(np.random.standard_normal((D, D)) / np.sqrt(D)),
        "b_up": f32(0.1 * np.random.standard_normal((D, 1))),
        "offs": striped(np.random.permutation(np.tile(np.arange(V), 2))[:N]),
    }


def reference(emb, pos_emb, norm_w, w_gate, b_gate, w_up, b_up, offs):
    idx = offs[:16].T.reshape(-1)
    h = f64(emb)[:, idx] + f64(pos_emb)
    x = h / np.sqrt(np.mean(h * h, axis=0, keepdims=True) + EPS) * f64(norm_w)
    a = f64(w_gate).T @ x + f64(b_gate)
    u = f64(w_up).T @ x + f64(b_up)
    return silu(a) * u + x

@@ -1,0 +1,91 @@
+import concourse.mybir as mybir
+from concourse.masks import make_identity
+
+F32 = mybir.dt.float32
+BF16 = mybir.dt.bfloat16
+U16 = mybir.dt.uint16
+ALU = mybir.AluOpType
+ACT = mybir.ActivationFunctionType
+
+P = 128
+D, V, N = 512, 1024, 128
+CB = D // P
+EPS = 1.1920928955078125e-07
+FLOPS = 2 * 2 * D * D * N
+
+
+def tile_repro_kernel(tc, emb, pos_emb, norm_w, w_gate, b_gate, w_up, b_up, offs, out):
+    nc = tc.nc
+    with (
+        tc.tile_pool(name="held", bufs=1) as held,
+        tc.psum_pool(name="psum", bufs=1) as psum,
+    ):
+        offsets = held.tile([P, N // 16], U16, name="offsets")
+        nc.sync.dma_start(offsets[:], offs)
+        pos = held.tile([P, CB, N], F32, name="pos")
+        nc.scalar.dma_start(pos[:], pos_emb.rearrange("(c p) j -> p c j", p=P))
+        tables = [held.tile([P, V], F32, name=f"table{c}") for c in range(CB)]
+        for c in range(CB):
+            queue = nc.sync if c % 2 == 0 else nc.scalar
+            queue.dma_start(tables[c][:], emb[c * P : (c + 1) * P, :])
+        gate_w = held.tile([P, CB, D], BF16, name="gate_w")
+        nc.sync.dma_start(gate_w[:], w_gate.rearrange("(c p) m -> p c m", p=P))
+        up_w = held.tile([P, CB, D], BF16, name="up_w")
+        nc.scalar.dma_start(up_w[:], w_up.rearrange("(c p) m -> p c m", p=P))
+
+        vec_rows = held.tile([3 * CB, P], F32, name="vec_rows")
+        for v, vec in enumerate((norm_w, b_gate, b_up)):
+            nc.gpsimd.dma_start(vec_rows[v * CB : (v + 1) * CB, :], vec.rearrange("(c p) o -> c (p o)", p=P))
+        ident = held.tile([3 * CB, 3 * CB], F32, name="ident")
+        make_identity(nc, ident[:])
+        vec_ps = psum.tile([P, 3 * CB], F32, name="vec_ps")
+        nc.tensor.matmul(vec_ps[:], vec_rows[:], ident[:], start=True, stop=True)
+        vec_cols = held.tile([P, 3 * CB], F32, name="vec_cols")
+        nc.vector.tensor_copy(vec_cols[:], vec_ps[:])
+        norm_col = [vec_cols[:, c : c + 1] for c in range(CB)]
+        gate_bias = [vec_cols[:, CB + m : CB + m + 1] for m in range(CB)]
+        up_bias = [vec_cols[:, 2 * CB + m : 2 * CB + m + 1] for m in range(CB)]
+
+        ones = held.tile([P, P], F32, name="ones")
+        nc.gpsimd.memset(ones[:], 1.0)
+        eps_col = held.tile([P, 1], F32, name="eps_col")
+        nc.gpsimd.memset(eps_col[:], EPS)
+
+        h = held.tile([P, CB, N], F32, name="h")
+        squares = held.tile([P, CB, N], F32, name="squares")
+        sum_ps = psum.tile([P, N], F32, name="sum_ps")
+        for c in range(CB):
+            nc.vector.tensor_tensor(h[:, c, :], tables[c][:].indirect(offsets[:]), pos[:, c, :], ALU.add)
+            nc.vector.tensor_tensor(squares[:, c, :], h[:, c, :], h[:, c, :], ALU.mult)
+            nc.tensor.matmul(sum_ps[:], ones[:], squares[:, c, :], start=(c == 0), stop=(c == CB - 1))
+
+        rms = held.tile([P, N], F32, name="rms")
+        nc.scalar.activation(rms[:], sum_ps[:], ACT.Sqrt, bias=eps_col[:], scale=1.0 / D)
+        r = held.tile([P, N], F32, name="r")
+        nc.vector.reciprocal(r[:], rms[:])
+
+        x_bf = held.tile([P, CB, N], BF16, name="x_bf")
+        x = held.tile([P, CB, N], F32, name="x")
+        for c in range(CB):
+            nc.vector.scalar_tensor_tensor(x_bf[:, c, :], h[:, c, :], norm_col[c], r[:], ALU.mult, ALU.mult)
+        for c in range(CB):
+            nc.vector.scalar_tensor_tensor(x[:, c, :], h[:, c, :], norm_col[c], r[:], ALU.mult, ALU.mult)
+
+        gate_ps = psum.tile([P, CB, N], F32, name="gate_ps")
+        for m in range(CB):
+            for c in range(CB):
+                nc.tensor.matmul(
+                    gate_ps[:, m, :], gate_w[:, c, m * P : (m + 1) * P], x_bf[:, c, :], start=(c == 0), stop=(c == CB - 1)
+                )
+        gated = held.tile([P, CB, N], F32, name="gated")
+        for m in range(CB):
+            nc.scalar.activation(gated[:, m, :], gate_ps[:, m, :], ACT.Silu, bias=gate_bias[m])
+
+        for m in range(CB):
+            up_ps = psum.tile([P, N], F32, name=f"up_ps{m}")
+            for c in range(CB):
+                nc.tensor.matmul(up_ps[:], up_w[:, c, m * P : (m + 1) * P], x_bf[:, c, :], start=(c == 0), stop=(c == CB - 1))
+            result = held.tile([P, N], F32, name=f"result{m}")
+            nc.vector.scalar_tensor_tensor(result[:], up_ps[:], up_bias[m], gated[:, m, :], ALU.add, ALU.mult)
+            nc.vector.tensor_tensor(result[:], result[:], x[:, m, :], ALU.add)
+            nc.sync.dma_start(out[m * P : (m + 1) * P, :], result[:])

@@ -1,5 +1,4 @@
 import concourse.mybir as mybir
-from concourse.masks import make_identity
 
 F32 = mybir.dt.float32
 BF16 = mybir.dt.bfloat16
@@ -12,6 +11,7 @@ D, V, N = 512, 1024, 128
 CB = D // P
 EPS = 1.1920928955078125e-07
 FLOPS = 2 * 2 * D * D * N
+FILL_LAST = 2
 
 
 def tile_repro_kernel(tc, emb, pos_emb, norm_w, w_gate, b_gate, w_up, b_up, offs, out):
@@ -23,33 +23,31 @@ def tile_repro_kernel(tc, emb, pos_emb, norm_w, w_gate, b_gate, w_up, b_up, offs
         offsets = held.tile([P, N // 16], U16, name="offsets")
         nc.sync.dma_start(offsets[:], offs)
         pos = held.tile([P, CB, N], F32, name="pos")
-        nc.scalar.dma_start(pos[:], pos_emb.rearrange("(c p) j -> p c j", p=P))
+        nc.sync.dma_start(pos[:], pos_emb.rearrange("(p c) j -> p c j", c=CB))
         tables = [held.tile([P, V], F32, name=f"table{c}") for c in range(CB)]
-        for c in range(CB):
-            queue = nc.sync if c % 2 == 0 else nc.scalar
-            queue.dma_start(tables[c][:], emb[c * P : (c + 1) * P, :])
+        emb_blocks = emb.rearrange("(p c) v -> c p v", c=CB)
+        nc.sync.dma_start(tables[0][:], emb_blocks[0])
+        norm_cols = held.tile([P, CB], F32, name="norm_cols")
+        gate_bias = held.tile([P, CB], F32, name="gate_bias")
+        up_bias = held.tile([P, CB], F32, name="up_bias")
+        for cols, vec in ((norm_cols, norm_w), (gate_bias, b_gate), (up_bias, b_up)):
+            nc.sync.dma_start(cols[:], vec.rearrange("(p c) o -> p (c o)", c=CB))
+        for c in range(1, CB):
+            nc.sync.dma_start(tables[c][:], emb_blocks[c])
         gate_w = held.tile([P, CB, D], BF16, name="gate_w")
-        nc.sync.dma_start(gate_w[:], w_gate.rearrange("(c p) m -> p c m", p=P))
+        nc.sync.dma_start(gate_w[:], w_gate.rearrange("(p c) m -> p c m", c=CB))
         up_w = held.tile([P, CB, D], BF16, name="up_w")
-        nc.scalar.dma_start(up_w[:], w_up.rearrange("(c p) m -> p c m", p=P))
-
-        vec_rows = held.tile([3 * CB, P], F32, name="vec_rows")
-        for v, vec in enumerate((norm_w, b_gate, b_up)):
-            nc.gpsimd.dma_start(vec_rows[v * CB : (v + 1) * CB, :], vec.rearrange("(c p) o -> c (p o)", p=P))
-        ident = held.tile([3 * CB, 3 * CB], F32, name="ident")
-        make_identity(nc, ident[:])
-        vec_ps = psum.tile([P, 3 * CB], F32, name="vec_ps")
-        nc.tensor.matmul(vec_ps[:], vec_rows[:], ident[:], start=True, stop=True)
-        vec_cols = held.tile([P, 3 * CB], F32, name="vec_cols")
-        nc.vector.tensor_copy(vec_cols[:], vec_ps[:])
-        norm_col = [vec_cols[:, c : c + 1] for c in range(CB)]
-        gate_bias = [vec_cols[:, CB + m : CB + m + 1] for m in range(CB)]
-        up_bias = [vec_cols[:, 2 * CB + m : 2 * CB + m + 1] for m in range(CB)]
+        nc.sync.dma_start(up_w[:], w_up.rearrange("(p c) m -> p c m", c=CB))
 
         ones = held.tile([P, P], F32, name="ones")
-        nc.gpsimd.memset(ones[:], 1.0)
+        nc.vector.memset(ones[:], 1.0)
         eps_col = held.tile([P, 1], F32, name="eps_col")
-        nc.gpsimd.memset(eps_col[:], EPS)
+        nc.vector.memset(eps_col[:], EPS)
+
+        table_warmer = held.tile([P, 2], F32, name="table_warmer")
+        nc.scalar.activation(table_warmer[:, 0:1], eps_col[:], ACT.Sqrt)
+
+        filler_ps = psum.tile([P, N], F32, name="filler_ps")
 
         h = held.tile([P, CB, N], F32, name="h")
         squares = held.tile([P, CB, N], F32, name="squares")
@@ -58,34 +56,39 @@ def tile_repro_kernel(tc, emb, pos_emb, norm_w, w_gate, b_gate, w_up, b_up, offs
             nc.vector.tensor_tensor(h[:, c, :], tables[c][:].indirect(offsets[:]), pos[:, c, :], ALU.add)
             nc.vector.tensor_tensor(squares[:, c, :], h[:, c, :], h[:, c, :], ALU.mult)
             nc.tensor.matmul(sum_ps[:], ones[:], squares[:, c, :], start=(c == 0), stop=(c == CB - 1))
+            for i in range(1 if c < CB - 1 else FILL_LAST):
+                nc.tensor.matmul(filler_ps[:], ones[:], squares[:, c, :], start=True, stop=True)
 
         rms = held.tile([P, N], F32, name="rms")
         nc.scalar.activation(rms[:], sum_ps[:], ACT.Sqrt, bias=eps_col[:], scale=1.0 / D)
         r = held.tile([P, N], F32, name="r")
         nc.vector.reciprocal(r[:], rms[:])
+        nc.scalar.activation(table_warmer[:, 1:2], rms[:, 0:1], ACT.Silu)
 
         x_bf = held.tile([P, CB, N], BF16, name="x_bf")
         x = held.tile([P, CB, N], F32, name="x")
         for c in range(CB):
-            nc.vector.scalar_tensor_tensor(x_bf[:, c, :], h[:, c, :], norm_col[c], r[:], ALU.mult, ALU.mult)
+            nc.vector.scalar_tensor_tensor(x_bf[:, c, :], h[:, c, :], norm_cols[:, c : c + 1], r[:], ALU.mult, ALU.mult)
         for c in range(CB):
-            nc.vector.scalar_tensor_tensor(x[:, c, :], h[:, c, :], norm_col[c], r[:], ALU.mult, ALU.mult)
+            nc.vector.scalar_tensor_tensor(x[:, c, :], h[:, c, :], norm_cols[:, c : c + 1], r[:], ALU.mult, ALU.mult)
+
+        gate_cols = gate_w[:].rearrange("p c (q m) -> p c m q", m=CB)
+        up_cols = up_w[:].rearrange("p c (q m) -> p c m q", m=CB)
+        out_blocks = out.rearrange("(q m) j -> m q j", m=CB)
 
         gate_ps = psum.tile([P, CB, N], F32, name="gate_ps")
         for m in range(CB):
             for c in range(CB):
-                nc.tensor.matmul(
-                    gate_ps[:, m, :], gate_w[:, c, m * P : (m + 1) * P], x_bf[:, c, :], start=(c == 0), stop=(c == CB - 1)
-                )
+                nc.tensor.matmul(gate_ps[:, m, :], gate_cols[:, c, m, :], x_bf[:, c, :], start=(c == 0), stop=(c == CB - 1))
         gated = held.tile([P, CB, N], F32, name="gated")
         for m in range(CB):
-            nc.scalar.activation(gated[:, m, :], gate_ps[:, m, :], ACT.Silu, bias=gate_bias[m])
+            nc.scalar.activation(gated[:, m, :], gate_ps[:, m, :], ACT.Silu, bias=gate_bias[:, m : m + 1])
 
         for m in range(CB):
             up_ps = psum.tile([P, N], F32, name=f"up_ps{m}")
             for c in range(CB):
-                nc.tensor.matmul(up_ps[:], up_w[:, c, m * P : (m + 1) * P], x_bf[:, c, :], start=(c == 0), stop=(c == CB - 1))
+                nc.tensor.matmul(up_ps[:], up_cols[:, c, m, :], x_bf[:, c, :], start=(c == 0), stop=(c == CB - 1))
             result = held.tile([P, N], F32, name=f"result{m}")
-            nc.vector.scalar_tensor_tensor(result[:], up_ps[:], up_bias[m], gated[:, m, :], ALU.add, ALU.mult)
+            nc.vector.scalar_tensor_tensor(result[:], up_ps[:], up_bias[:, m : m + 1], gated[:, m, :], ALU.add, ALU.mult)
             nc.vector.tensor_tensor(result[:], result[:], x[:, m, :], ALU.add)
-            nc.sync.dma_start(out[m * P : (m + 1) * P, :], result[:])
+            nc.sync.dma_start(out_blocks[m], result[:])

@@ -45,7 +45,7 @@ def tile_repro_kernel(tc, emb, pos_emb, norm_w, w_gate, b_gate, w_up, b_up, offs
         nc.vector.memset(eps_col[:], EPS)
 
         table_warmer = held.tile([P, 2], F32, name="table_warmer")
-        nc.scalar.activation(table_warmer[:, 0:1], eps_col[:], ACT.Sqrt)
+        nc.scalar.activation(table_warmer[:, 0:1], eps_col[:], ACT.Abs_reciprocal_sqrt)
 
         filler_ps = psum.tile([P, N], F32, name="filler_ps")
 
@@ -59,11 +59,9 @@ def tile_repro_kernel(tc, emb, pos_emb, norm_w, w_gate, b_gate, w_up, b_up, offs
             for i in range(1 if c < CB - 1 else FILL_LAST):
                 nc.tensor.matmul(filler_ps[:], ones[:], squares[:, c, :], start=True, stop=True)
 
-        rms = held.tile([P, N], F32, name="rms")
-        nc.scalar.activation(rms[:], sum_ps[:], ACT.Sqrt, bias=eps_col[:], scale=1.0 / D)
         r = held.tile([P, N], F32, name="r")
-        nc.vector.reciprocal(r[:], rms[:])
-        nc.scalar.activation(table_warmer[:, 1:2], rms[:, 0:1], ACT.Silu)
+        nc.scalar.activation(r[:], sum_ps[:], ACT.Abs_reciprocal_sqrt, bias=eps_col[:], scale=1.0 / D)
+        nc.scalar.activation(table_warmer[:, 1:2], r[:, 0:1], ACT.Silu)
 
         x_bf = held.tile([P, CB, N], BF16, name="x_bf")
         x = held.tile([P, CB, N], F32, name="x")

@@ -1,4 +1,5 @@
 import concourse.mybir as mybir
+from concourse.masks import make_identity
 
 F32 = mybir.dt.float32
 BF16 = mybir.dt.bfloat16
@@ -23,26 +24,33 @@ def tile_repro_kernel(tc, emb, pos_emb, norm_w, w_gate, b_gate, w_up, b_up, offs
         offsets = held.tile([P, N // 16], U16, name="offsets")
         nc.sync.dma_start(offsets[:], offs)
         pos = held.tile([P, CB, N], F32, name="pos")
-        nc.sync.dma_start(pos[:], pos_emb.rearrange("(p c) j -> p c j", c=CB))
+        nc.sync.dma_start(pos[:], pos_emb.rearrange("(c p) j -> p c j", p=P))
         tables = [held.tile([P, V], F32, name=f"table{c}") for c in range(CB)]
-        emb_blocks = emb.rearrange("(p c) v -> c p v", c=CB)
-        nc.sync.dma_start(tables[0][:], emb_blocks[0])
-        norm_cols = held.tile([P, CB], F32, name="norm_cols")
-        gate_bias = held.tile([P, CB], F32, name="gate_bias")
-        up_bias = held.tile([P, CB], F32, name="up_bias")
-        for cols, vec in ((norm_cols, norm_w), (gate_bias, b_gate), (up_bias, b_up)):
-            nc.sync.dma_start(cols[:], vec.rearrange("(p c) o -> p (c o)", c=CB))
+        nc.sync.dma_start(tables[0][:], emb[0:P, :])
+        vec_rows = held.tile([3 * CB, P], F32, name="vec_rows")
+        for v, vec in enumerate((norm_w, b_gate, b_up)):
+            nc.sync.dma_start(vec_rows[v * CB : (v + 1) * CB, :], vec.rearrange("(c p) o -> c (p o)", p=P))
         for c in range(1, CB):
-            nc.sync.dma_start(tables[c][:], emb_blocks[c])
+            nc.sync.dma_start(tables[c][:], emb[c * P : (c + 1) * P, :])
         gate_w = held.tile([P, CB, D], BF16, name="gate_w")
-        nc.sync.dma_start(gate_w[:], w_gate.rearrange("(p c) m -> p c m", c=CB))
+        nc.sync.dma_start(gate_w[:], w_gate.rearrange("(c p) m -> p c m", p=P))
         up_w = held.tile([P, CB, D], BF16, name="up_w")
-        nc.sync.dma_start(up_w[:], w_up.rearrange("(p c) m -> p c m", c=CB))
+        nc.sync.dma_start(up_w[:], w_up.rearrange("(c p) m -> p c m", p=P))
 
         ones = held.tile([P, P], F32, name="ones")
         nc.vector.memset(ones[:], 1.0)
         eps_col = held.tile([P, 1], F32, name="eps_col")
         nc.vector.memset(eps_col[:], EPS)
+
+        ident = held.tile([3 * CB, 3 * CB], F32, name="ident")
+        make_identity(nc, ident[:])
+        vec_ps = psum.tile([P, 3 * CB], F32, name="vec_ps")
+        nc.tensor.matmul(vec_ps[:], vec_rows[:], ident[:], start=True, stop=True)
+        vec_cols = held.tile([P, 3 * CB], F32, name="vec_cols")
+        nc.vector.tensor_copy(vec_cols[:], vec_ps[:])
+        norm_cols = vec_cols[:, 0:CB]
+        gate_bias = vec_cols[:, CB : 2 * CB]
+        up_bias = vec_cols[:, 2 * CB : 3 * CB]
 
         table_warmer = held.tile([P, 2], F32, name="table_warmer")
         nc.scalar.activation(table_warmer[:, 0:1], eps_col[:], ACT.Abs_reciprocal_sqrt)
@@ -70,14 +78,10 @@ def tile_repro_kernel(tc, emb, pos_emb, norm_w, w_gate, b_gate, w_up, b_up, offs
         for c in range(CB):
             nc.vector.scalar_tensor_tensor(x[:, c, :], h[:, c, :], norm_cols[:, c : c + 1], r[:], ALU.mult, ALU.mult)
 
-        gate_cols = gate_w[:].rearrange("p c (q m) -> p c m q", m=CB)
-        up_cols = up_w[:].rearrange("p c (q m) -> p c m q", m=CB)
-        out_blocks = out.rearrange("(q m) j -> m q j", m=CB)
-
         gate_ps = psum.tile([P, CB, N], F32, name="gate_ps")
         for m in range(CB):
             for c in range(CB):
-                nc.tensor.matmul(gate_ps[:, m, :], gate_cols[:, c, m, :], x_bf[:, c, :], start=(c == 0), stop=(c == CB - 1))
+                nc.tensor.matmul(gate_ps[:, m, :], gate_w[:, c, m * P : (m + 1) * P], x_bf[:, c, :], start=(c == 0), stop=(c == CB - 1))
         gated = held.tile([P, CB, N], F32, name="gated")
         for m in range(CB):
             nc.scalar.activation(gated[:, m, :], gate_ps[:, m, :], ACT.Silu, bias=gate_bias[:, m : m + 1])
@@ -85,8 +89,8 @@ def tile_repro_kernel(tc, emb, pos_emb, norm_w, w_gate, b_gate, w_up, b_up, offs
         for m in range(CB):
             up_ps = psum.tile([P, N], F32, name=f"up_ps{m}")
             for c in range(CB):
-                nc.tensor.matmul(up_ps[:], up_cols[:, c, m, :], x_bf[:, c, :], start=(c == 0), stop=(c == CB - 1))
+                nc.tensor.matmul(up_ps[:], up_w[:, c, m * P : (m + 1) * P], x_bf[:, c, :], start=(c == 0), stop=(c == CB - 1))
             result = held.tile([P, N], F32, name=f"result{m}")
             nc.vector.scalar_tensor_tensor(result[:], up_ps[:], up_bias[:, m : m + 1], gated[:, m, :], ALU.add, ALU.mult)
             nc.vector.tensor_tensor(result[:], result[:], x[:, m, :], ALU.add)
-            nc.sync.dma_start(out_blocks[m], result[:])
+            nc.sync.dma_start(out[m * P : (m + 1) * P, :], result[:])

@@ -1,5 +1,4 @@
 import concourse.mybir as mybir
-from concourse.masks import make_identity
 
 F32 = mybir.dt.float32
 BF16 = mybir.dt.bfloat16
@@ -24,33 +23,25 @@ def tile_repro_kernel(tc, emb, pos_emb, norm_w, w_gate, b_gate, w_up, b_up, offs
         offsets = held.tile([P, N // 16], U16, name="offsets")
         nc.sync.dma_start(offsets[:], offs)
         pos = held.tile([P, CB, N], F32, name="pos")
-        nc.sync.dma_start(pos[:], pos_emb.rearrange("(c p) j -> p c j", p=P))
+        nc.sync.dma_start(pos[:], pos_emb.rearrange("(p c) j -> p c j", c=CB))
         tables = [held.tile([P, V], F32, name=f"table{c}") for c in range(CB)]
-        nc.sync.dma_start(tables[0][:], emb[0:P, :])
-        vec_rows = held.tile([3 * CB, P], F32, name="vec_rows")
-        for v, vec in enumerate((norm_w, b_gate, b_up)):
-            nc.sync.dma_start(vec_rows[v * CB : (v + 1) * CB, :], vec.rearrange("(c p) o -> c (p o)", p=P))
-        for c in range(1, CB):
-            nc.sync.dma_start(tables[c][:], emb[c * P : (c + 1) * P, :])
+        emb_blocks = emb.rearrange("(p c) v -> c p v", c=CB)
+        for c in range(CB):
+            nc.sync.dma_start(tables[c][:], emb_blocks[c])
+        norm_cols = held.tile([P, CB], F32, name="norm_cols")
+        gate_bias = held.tile([P, CB], F32, name="gate_bias")
+        up_bias = held.tile([P, CB], F32, name="up_bias")
+        for cols, vec in ((norm_cols, norm_w), (gate_bias, b_gate), (up_bias, b_up)):
+            nc.sync.dma_start(cols[:], vec.rearrange("(p c) o -> p (c o)", c=CB))
         gate_w = held.tile([P, CB, D], BF16, name="gate_w")
-        nc.sync.dma_start(gate_w[:], w_gate.rearrange("(c p) m -> p c m", p=P))
+        nc.sync.dma_start(gate_w[:], w_gate.rearrange("(p c) m -> p c m", c=CB))
         up_w = held.tile([P, CB, D], BF16, name="up_w")
-        nc.sync.dma_start(up_w[:], w_up.rearrange("(c p) m -> p c m", p=P))
+        nc.sync.dma_start(up_w[:], w_up.rearrange("(p c) m -> p c m", c=CB))
 
         ones = held.tile([P, P], F32, name="ones")
         nc.vector.memset(ones[:], 1.0)
         eps_col = held.tile([P, 1], F32, name="eps_col")
         nc.vector.memset(eps_col[:], EPS)
-
-        ident = held.tile([3 * CB, 3 * CB], F32, name="ident")
-        make_identity(nc, ident[:])
-        vec_ps = psum.tile([P, 3 * CB], F32, name="vec_ps")
-        nc.tensor.matmul(vec_ps[:], vec_rows[:], ident[:], start=True, stop=True)
-        vec_cols = held.tile([P, 3 * CB], F32, name="vec_cols")
-        nc.vector.tensor_copy(vec_cols[:], vec_ps[:])
-        norm_cols = vec_cols[:, 0:CB]
-        gate_bias = vec_cols[:, CB : 2 * CB]
-        up_bias = vec_cols[:, 2 * CB : 3 * CB]
 
         table_warmer = held.tile([P, 2], F32, name="table_warmer")
         nc.scalar.activation(table_warmer[:, 0:1], eps_col[:], ACT.Abs_reciprocal_sqrt)
@@ -78,10 +69,14 @@ def tile_repro_kernel(tc, emb, pos_emb, norm_w, w_gate, b_gate, w_up, b_up, offs
         for c in range(CB):
             nc.vector.scalar_tensor_tensor(x[:, c, :], h[:, c, :], norm_cols[:, c : c + 1], r[:], ALU.mult, ALU.mult)
 
+        gate_cols = gate_w[:].rearrange("p c (q m) -> p c m q", m=CB)
+        up_cols = up_w[:].rearrange("p c (q m) -> p c m q", m=CB)
+        out_blocks = out.rearrange("(q m) j -> m q j", m=CB)
+
         gate_ps = psum.tile([P, CB, N], F32, name="gate_ps")
         for m in range(CB):
             for c in range(CB):
-                nc.tensor.matmul(gate_ps[:, m, :], gate_w[:, c, m * P : (m + 1) * P], x_bf[:, c, :], start=(c == 0), stop=(c == CB - 1))
+                nc.tensor.matmul(gate_ps[:, m, :], gate_cols[:, c, m, :], x_bf[:, c, :], start=(c == 0), stop=(c == CB - 1))
         gated = held.tile([P, CB, N], F32, name="gated")
         for m in range(CB):
             nc.scalar.activation(gated[:, m, :], gate_ps[:, m, :], ACT.Silu, bias=gate_bias[:, m : m + 1])
@@ -89,8 +84,8 @@ def tile_repro_kernel(tc, emb, pos_emb, norm_w, w_gate, b_gate, w_up, b_up, offs
         for m in range(CB):
             up_ps = psum.tile([P, N], F32, name=f"up_ps{m}")
             for c in range(CB):
-                nc.tensor.matmul(up_ps[:], up_w[:, c, m * P : (m + 1) * P], x_bf[:, c, :], start=(c == 0), stop=(c == CB - 1))
+                nc.tensor.matmul(up_ps[:], up_cols[:, c, m, :], x_bf[:, c, :], start=(c == 0), stop=(c == CB - 1))
             result = held.tile([P, N], F32, name=f"result{m}")
             nc.vector.scalar_tensor_tensor(result[:], up_ps[:], up_bias[:, m : m + 1], gated[:, m, :], ALU.add, ALU.mult)
             nc.vector.tensor_tensor(result[:], result[:], x[:, m, :], ALU.add)
-            nc.sync.dma_start(out[m * P : (m + 1) * P, :], result[:])
+            nc.sync.dma_start(out_blocks[m], result[:])

@@ -11,7 +11,6 @@ D, V, N = 512, 1024, 128
 CB = D // P
 EPS = 1.1920928955078125e-07
 FLOPS = 2 * 2 * D * D * N
-FILL_LAST = 2
 
 
 def tile_repro_kernel(tc, emb, pos_emb, norm_w, w_gate, b_gate, w_up, b_up, offs, out):
@@ -40,11 +39,9 @@ def tile_repro_kernel(tc, emb, pos_emb, norm_w, w_gate, b_gate, w_up, b_up, offs
 
         ones = held.tile([P, P], F32, name="ones")
         nc.vector.memset(ones[:], 1.0)
-        eps_col = held.tile([P, 1], F32, name="eps_col")
-        nc.vector.memset(eps_col[:], EPS)
 
         table_warmer = held.tile([P, 2], F32, name="table_warmer")
-        nc.scalar.activation(table_warmer[:, 0:1], eps_col[:], ACT.Abs_reciprocal_sqrt)
+        nc.scalar.activation(table_warmer[:, 0:1], ones[:, 0:1], ACT.Abs_reciprocal_sqrt)
 
         filler_ps = psum.tile([P, N], F32, name="filler_ps")
 
@@ -55,11 +52,10 @@ def tile_repro_kernel(tc, emb, pos_emb, norm_w, w_gate, b_gate, w_up, b_up, offs
             nc.vector.tensor_tensor(h[:, c, :], tables[c][:].indirect(offsets[:]), pos[:, c, :], ALU.add)
             nc.vector.tensor_tensor(squares[:, c, :], h[:, c, :], h[:, c, :], ALU.mult)
             nc.tensor.matmul(sum_ps[:], ones[:], squares[:, c, :], start=(c == 0), stop=(c == CB - 1))
-            for i in range(1 if c < CB - 1 else FILL_LAST):
-                nc.tensor.matmul(filler_ps[:], ones[:], squares[:, c, :], start=True, stop=True)
+            nc.tensor.matmul(filler_ps[:], ones[:], squares[:, c, :], start=True, stop=True)
 
         r = held.tile([P, N], F32, name="r")
-        nc.scalar.activation(r[:], sum_ps[:], ACT.Abs_reciprocal_sqrt, bias=eps_col[:], scale=1.0 / D)
+        nc.scalar.activation(r[:], sum_ps[:], ACT.Abs_reciprocal_sqrt, bias=EPS, scale=1.0 / D)
         nc.scalar.activation(table_warmer[:, 1:2], r[:, 0:1], ACT.Silu)
 
         x_bf = held.tile([P, CB, N], BF16, name="x_bf")

@@ -69,13 +69,15 @@ def tile_repro_kernel(tc, emb, pos_emb, norm_w, w_gate, b_gate, w_up, b_up, offs
         up_cols = up_w[:].rearrange("p c (q m) -> p c m q", m=CB)
         out_blocks = out.rearrange("(q m) j -> m q j", m=CB)
 
-        gate_ps = psum.tile([P, CB, N], F32, name="gate_ps")
-        for m in range(CB):
+        gate_ps = [psum.tile([P, CB // 2, N], F32, name=f"gate_ps{b}") for b in range(2)]
+        for pair in range(CB // 2):
             for c in range(CB):
-                nc.tensor.matmul(gate_ps[:, m, :], gate_cols[:, c, m, :], x_bf[:, c, :], start=(c == 0), stop=(c == CB - 1))
+                for b in range(2):
+                    m = 2 * pair + b
+                    nc.tensor.matmul(gate_ps[b][:, pair, :], gate_cols[:, c, m, :], x_bf[:, c, :], start=(c == 0), stop=(c == CB - 1))
         gated = held.tile([P, CB, N], F32, name="gated")
         for m in range(CB):
-            nc.scalar.activation(gated[:, m, :], gate_ps[:, m, :], ACT.Silu, bias=gate_bias[:, m : m + 1])
+            nc.scalar.activation(gated[:, m, :], gate_ps[m % 2][:, m // 2, :], ACT.Silu, bias=gate_bias[:, m : m + 1])
 
         for m in range(CB):
             up_ps = psum.tile([P, N], F32, name=f"up_ps{m}")

@@ -11,6 +11,7 @@ D, V, N = 512, 1024, 128
 CB = D // P
 EPS = 1.1920928955078125e-07
 FLOPS = 2 * 2 * D * D * N
+EARLY_FILLERS = 2 * CB
 
 
 def tile_repro_kernel(tc, emb, pos_emb, norm_w, w_gate, b_gate, w_up, b_up, offs, out):
@@ -44,6 +45,8 @@ def tile_repro_kernel(tc, emb, pos_emb, norm_w, w_gate, b_gate, w_up, b_up, offs
         nc.scalar.activation(table_warmer[:, 0:1], ones[:, 0:1], ACT.Abs_reciprocal_sqrt)
 
         filler_ps = psum.tile([P, N], F32, name="filler_ps")
+        for early in range(EARLY_FILLERS):
+            nc.tensor.matmul(filler_ps[:], ones[:], ones[:], start=True, stop=True)
 
         h = held.tile([P, CB, N], F32, name="h")
         squares = held.tile([P, CB, N], F32, name="squares")

@@ -11,6 +11,7 @@ D, V, N = 512, 1024, 128
 CB = D // P
 EPS = 1.1920928955078125e-07
 FLOPS = 2 * 2 * D * D * N
+HALVES = [slice(0, N // 2), slice(N // 2, N)]
 EARLY_FILLERS = 2 * CB
 
 
@@ -50,21 +51,26 @@ def tile_repro_kernel(tc, emb, pos_emb, norm_w, w_gate, b_gate, w_up, b_up, offs
 
         h = held.tile([P, CB, N], F32, name="h")
         squares = held.tile([P, CB, N], F32, name="squares")
-        sum_ps = psum.tile([P, N], F32, name="sum_ps")
+        sum_ps = [psum.tile([P, N], F32, name=f"sum_ps{k}") for k in range(len(HALVES))]
         for c in range(CB):
-            nc.vector.tensor_tensor(h[:, c, :], tables[c][:].indirect(offsets[:]), pos[:, c, :], ALU.add)
-            nc.vector.tensor_tensor(squares[:, c, :], h[:, c, :], h[:, c, :], ALU.mult)
-            nc.tensor.matmul(sum_ps[:], ones[:], squares[:, c, :], start=(c == 0), stop=(c == CB - 1))
+            for tokens in HALVES if c == CB - 1 else [slice(0, N)]:
+                list_part = offsets[:, tokens.start // 16 : tokens.stop // 16]
+                nc.vector.tensor_tensor(h[:, c, tokens], tables[c][:].indirect(list_part), pos[:, c, tokens], ALU.add)
+                nc.scalar.activation(squares[:, c, tokens], h[:, c, tokens], ACT.Square)
+            for k, tokens in enumerate(HALVES):
+                nc.tensor.matmul(sum_ps[k][:, tokens], ones[:], squares[:, c, tokens], start=(c == 0), stop=(c == CB - 1))
             nc.tensor.matmul(filler_ps[:], ones[:], squares[:, c, :], start=True, stop=True)
 
         r = held.tile([P, N], F32, name="r")
-        nc.scalar.activation(r[:], sum_ps[:], ACT.Abs_reciprocal_sqrt, bias=EPS, scale=1.0 / D)
-        nc.scalar.activation(table_warmer[:, 1:2], r[:, 0:1], ACT.Silu)
+        for k, tokens in enumerate(HALVES):
+            nc.scalar.activation(r[:, tokens], sum_ps[k][:, tokens], ACT.Abs_reciprocal_sqrt, bias=EPS, scale=1.0 / D)
+        nc.scalar.activation(table_warmer[:, 1:2], r[:, N - 1 : N], ACT.Silu)
 
         x_bf = held.tile([P, CB, N], BF16, name="x_bf")
         x = held.tile([P, CB, N], F32, name="x")
-        for c in range(CB):
-            nc.vector.scalar_tensor_tensor(x_bf[:, c, :], h[:, c, :], norm_cols[:, c : c + 1], r[:], ALU.mult, ALU.mult)
+        for tokens in HALVES:
+            for c in range(CB):
+                nc.vector.scalar_tensor_tensor(x_bf[:, c, tokens], h[:, c, tokens], norm_cols[:, c : c + 1], r[:, tokens], ALU.mult, ALU.mult)
         for c in range(CB):
             nc.vector.scalar_tensor_tensor(x[:, c, :], h[:, c, :], norm_cols[:, c : c + 1], r[:], ALU.mult, ALU.mult)
 
@@ -72,21 +78,24 @@ def tile_repro_kernel(tc, emb, pos_emb, norm_w, w_gate, b_gate, w_up, b_up, offs
         up_cols = up_w[:].rearrange("p c (q m) -> p c m q", m=CB)
         out_blocks = out.rearrange("(q m) j -> m q j", m=CB)
 
-        gate_ps = [psum.tile([P, CB // 2, N], F32, name=f"gate_ps{b}") for b in range(2)]
-        for pair in range(CB // 2):
+        gate_ps = [psum.tile([P, N], F32, name=f"gate_ps{m}") for m in range(CB)]
+        for tokens in HALVES:
             for c in range(CB):
-                for b in range(2):
-                    m = 2 * pair + b
-                    nc.tensor.matmul(gate_ps[b][:, pair, :], gate_cols[:, c, m, :], x_bf[:, c, :], start=(c == 0), stop=(c == CB - 1))
+                for m in range(CB):
+                    nc.tensor.matmul(gate_ps[m][:, tokens], gate_cols[:, c, m, :], x_bf[:, c, tokens], start=(c == 0), stop=(c == CB - 1))
         gated = held.tile([P, CB, N], F32, name="gated")
         for m in range(CB):
-            nc.scalar.activation(gated[:, m, :], gate_ps[m % 2][:, m // 2, :], ACT.Silu, bias=gate_bias[:, m : m + 1])
+            nc.scalar.activation(gated[:, m, :], gate_ps[m][:], ACT.Silu, bias=gate_bias[:, m : m + 1])
 
-        for m in range(CB):
-            up_ps = psum.tile([P, N], F32, name=f"up_ps{m}")
+        up_groups = [(m, slice(0, N)) for m in range(CB - 1)] + [(CB - 1, tokens) for tokens in HALVES]
+        up_banks = ["up_ps", "filler_ps", "sum_ps0", "sum_ps1", "gate_ps0"]
+        results = [held.tile([P, N], F32, name=f"result{m}") for m in range(CB)]
+        for (m, tokens), bank in zip(up_groups, up_banks):
+            up_ps = psum.tile([P, N], F32, name="up_ps", tag=bank)
             for c in range(CB):
-                nc.tensor.matmul(up_ps[:], up_cols[:, c, m, :], x_bf[:, c, :], start=(c == 0), stop=(c == CB - 1))
-            result = held.tile([P, N], F32, name=f"result{m}")
-            nc.vector.scalar_tensor_tensor(result[:], up_ps[:], up_bias[:, m : m + 1], gated[:, m, :], ALU.add, ALU.mult)
-            nc.vector.tensor_tensor(result[:], result[:], x[:, m, :], ALU.add)
-            nc.sync.dma_start(out_blocks[m], result[:])
+                nc.tensor.matmul(up_ps[:, tokens], up_cols[:, c, m, :], x_bf[:, c, tokens], start=(c == 0), stop=(c == CB - 1))
+            result = results[m][:, tokens]
+            nc.vector.scalar_tensor_tensor(result, up_ps[:, tokens], up_bias[:, m : m + 1], gated[:, m, tokens], ALU.add, ALU.mult)
+            nc.vector.tensor_tensor(result, result, x[:, m, tokens], ALU.add)
+        for m in range(CB):
+            nc.sync.dma_start(out_blocks[m], results[m][:])

@@ -79,10 +79,11 @@ def tile_repro_kernel(tc, emb, pos_emb, norm_w, w_gate, b_gate, w_up, b_up, offs
         out_blocks = out.rearrange("(q m) j -> m q j", m=CB)
 
         gate_ps = [psum.tile([P, N], F32, name=f"gate_ps{m}") for m in range(CB)]
-        for tokens in HALVES:
-            for c in range(CB):
-                for m in range(CB):
-                    nc.tensor.matmul(gate_ps[m][:, tokens], gate_cols[:, c, m, :], x_bf[:, c, tokens], start=(c == 0), stop=(c == CB - 1))
+        for pair, token_parts in (((0, 1), HALVES), ((2, 3), [slice(0, N)])):
+            for tokens in token_parts:
+                for c in range(CB):
+                    for m in pair:
+                        nc.tensor.matmul(gate_ps[m][:, tokens], gate_cols[:, c, m, :], x_bf[:, c, tokens], start=(c == 0), stop=(c == CB - 1))
         gated = held.tile([P, CB, N], F32, name="gated")
         for m in range(CB):
             nc.scalar.activation(gated[:, m, :], gate_ps[m][:], ACT.Silu, bias=gate_bias[:, m : m + 1])

@@ -24,7 +24,7 @@ def tile_repro_kernel(tc, emb, pos_emb, norm_w, w_gate, b_gate, w_up, b_up, offs
         offsets = held.tile([P, N // 16], U16, name="offsets")
         nc.sync.dma_start(offsets[:], offs)
         pos = held.tile([P, CB, N], F32, name="pos")
-        nc.sync.dma_start(pos[:], pos_emb.rearrange("(p c) j -> p c j", c=CB))
+        nc.scalar.dma_start(pos[:], pos_emb.rearrange("(p c) j -> p c j", c=CB))
         tables = [held.tile([P, V], F32, name=f"table{c}") for c in range(CB)]
         emb_blocks = emb.rearrange("(p c) v -> c p v", c=CB)
         for c in range(CB):

import concourse.mybir as mybir

F32 = mybir.dt.float32
BF16 = mybir.dt.bfloat16
U16 = mybir.dt.uint16
ALU = mybir.AluOpType
ACT = mybir.ActivationFunctionType

P = 128
D, V, N = 512, 1024, 128
CB = D // P
EPS = 1.1920928955078125e-07
FLOPS = 2 * 2 * D * D * N
HALVES = [slice(0, N // 2), slice(N // 2, N)]
EARLY_FILLERS = 2 * CB


def tile_repro_kernel(tc, emb, pos_emb, norm_w, w_gate, b_gate, w_up, b_up, offs, out):
    nc = tc.nc
    with (
        tc.tile_pool(name="held", bufs=1) as held,
        tc.psum_pool(name="psum", bufs=1) as psum,
    ):
        offsets = held.tile([P, N // 16], U16, name="offsets")
        nc.sync.dma_start(offsets[:], offs)
        pos = held.tile([P, CB, N], F32, name="pos")
        nc.scalar.dma_start(pos[:], pos_emb.rearrange("(p c) j -> p c j", c=CB))
        tables = [held.tile([P, V], F32, name=f"table{c}") for c in range(CB)]
        emb_blocks = emb.rearrange("(p c) v -> c p v", c=CB)
        for c in range(CB):
            nc.sync.dma_start(tables[c][:], emb_blocks[c])
        norm_cols = held.tile([P, CB], F32, name="norm_cols")
        gate_bias = held.tile([P, CB], F32, name="gate_bias")
        up_bias = held.tile([P, CB], F32, name="up_bias")
        for cols, vec in ((norm_cols, norm_w), (gate_bias, b_gate), (up_bias, b_up)):
            nc.sync.dma_start(cols[:], vec.rearrange("(p c) o -> p (c o)", c=CB))
        gate_w = held.tile([P, CB, D], BF16, name="gate_w")
        nc.sync.dma_start(gate_w[:], w_gate.rearrange("(p c) m -> p c m", c=CB))
        up_w = held.tile([P, CB, D], BF16, name="up_w")
        nc.sync.dma_start(up_w[:], w_up.rearrange("(p c) m -> p c m", c=CB))

        ones = held.tile([P, P], F32, name="ones")
        nc.vector.memset(ones[:], 1.0)

        table_warmer = held.tile([P, 2], F32, name="table_warmer")
        nc.scalar.activation(table_warmer[:, 0:1], ones[:, 0:1], ACT.Abs_reciprocal_sqrt)

        filler_ps = psum.tile([P, N], F32, name="filler_ps")
        for early in range(EARLY_FILLERS):
            nc.tensor.matmul(filler_ps[:], ones[:], ones[:], start=True, stop=True)

        h = held.tile([P, CB, N], F32, name="h")
        squares = held.tile([P, CB, N], F32, name="squares")
        sum_ps = [psum.tile([P, N], F32, name=f"sum_ps{k}") for k in range(len(HALVES))]
        for c in range(CB):
            for tokens in HALVES if c == CB - 1 else [slice(0, N)]:
                list_part = offsets[:, tokens.start // 16 : tokens.stop // 16]
                nc.vector.tensor_tensor(h[:, c, tokens], tables[c][:].indirect(list_part), pos[:, c, tokens], ALU.add)
                nc.scalar.activation(squares[:, c, tokens], h[:, c, tokens], ACT.Square)
            for k, tokens in enumerate(HALVES):
                nc.tensor.matmul(sum_ps[k][:, tokens], ones[:], squares[:, c, tokens], start=(c == 0), stop=(c == CB - 1))
            nc.tensor.matmul(filler_ps[:], ones[:], squares[:, c, :], start=True, stop=True)

        r = held.tile([P, N], F32, name="r")
        for k, tokens in enumerate(HALVES):
            nc.scalar.activation(r[:, tokens], sum_ps[k][:, tokens], ACT.Abs_reciprocal_sqrt, bias=EPS, scale=1.0 / D)
        nc.scalar.activation(table_warmer[:, 1:2], r[:, N - 1 : N], ACT.Silu)

        x_bf = held.tile([P, CB, N], BF16, name="x_bf")
        x = held.tile([P, CB, N], F32, name="x")
        for tokens in HALVES:
            for c in range(CB):
                nc.vector.scalar_tensor_tensor(x_bf[:, c, tokens], h[:, c, tokens], norm_cols[:, c : c + 1], r[:, tokens], ALU.mult, ALU.mult)
        for c in range(CB):
            nc.vector.scalar_tensor_tensor(x[:, c, :], h[:, c, :], norm_cols[:, c : c + 1], r[:], ALU.mult, ALU.mult)

        gate_cols = gate_w[:].rearrange("p c (q m) -> p c m q", m=CB)
        up_cols = up_w[:].rearrange("p c (q m) -> p c m q", m=CB)
        out_blocks = out.rearrange("(q m) j -> m q j", m=CB)

        gate_ps = [psum.tile([P, N], F32, name=f"gate_ps{m}") for m in range(CB)]
        for pair, token_parts in (((0, 1), HALVES), ((2, 3), [slice(0, N)])):
            for tokens in token_parts:
                for c in range(CB):
                    for m in pair:
                        nc.tensor.matmul(gate_ps[m][:, tokens], gate_cols[:, c, m, :], x_bf[:, c, tokens], start=(c == 0), stop=(c == CB - 1))
        gated = held.tile([P, CB, N], F32, name="gated")
        for m in range(CB):
            nc.scalar.activation(gated[:, m, :], gate_ps[m][:], ACT.Silu, bias=gate_bias[:, m : m + 1])

        up_groups = [(m, slice(0, N)) for m in range(CB - 1)] + [(CB - 1, tokens) for tokens in HALVES]
        up_banks = ["up_ps", "filler_ps", "sum_ps0", "sum_ps1", "gate_ps0"]
        results = [held.tile([P, N], F32, name=f"result{m}") for m in range(CB)]
        for (m, tokens), bank in zip(up_groups, up_banks):
            up_ps = psum.tile([P, N], F32, name="up_ps", tag=bank)
            for c in range(CB):
                nc.tensor.matmul(up_ps[:, tokens], up_cols[:, c, m, :], x_bf[:, c, tokens], start=(c == 0), stop=(c == CB - 1))
            result = results[m][:, tokens]
            nc.vector.scalar_tensor_tensor(result, up_ps[:, tokens], up_bias[:, m : m + 1], gated[:, m, tokens], ALU.add, ALU.mult)
            nc.vector.tensor_tensor(result, result, x[:, m, tokens], ALU.add)
        for m in range(CB):
            nc.sync.dma_start(out_blocks[m], results[m][:])
